import numpy as np
import ml_dtypes


def mxq(x, axis, fmt="e4m3"):
    dtype, down = {"e4m3": (ml_dtypes.float8_e4m3fn, 7), "e5m2": (ml_dtypes.float8_e5m2, 14)}[fmt]
    v = np.moveaxis(np.asarray(x, np.float32).astype(ml_dtypes.bfloat16).astype(np.float64), axis, -1)
    blocks = v.reshape(v.shape[:-1] + (-1, 32))
    amax = np.abs(blocks).max(-1, keepdims=True)
    byte = np.maximum(np.where(amax > 0, np.frexp(amax)[1] - 1 + 127, 0) - down, 1)
    scale = np.exp2(byte - 127.0)
    codes = (blocks / scale).astype(np.float32).astype(dtype).astype(np.float64)
    return np.moveaxis((codes * scale).reshape(v.shape), -1, axis)


WIDE = False


def mx_kscale(k):
    if not WIDE:
        return np.ones(k)
    levels = np.array([10, -10, 5, -5, 0])
    a = np.random.permutation(np.resize(levels, k // 512 * 4)).reshape(k // 512, 4)
    idx = np.arange(k)
    return np.exp2(a[idx // 512, idx % 128 // 32])


BF16 = ml_dtypes.bfloat16


def bf(x):
    return np.asarray(x, np.float32).astype(BF16)


def f64(x):
    return np.asarray(x).astype(np.float64)


C, K, D = 200, 16, 512
B = 1024
LOG_2PI = float(np.log(2.0 * np.pi))


def softmax(v, axis):
    e = np.exp(v - v.max(axis=axis, keepdims=True))
    return e / e.sum(axis=axis, keepdims=True)


def logsumexp(v, axis, keepdims=False):
    m = v.max(axis=axis, keepdims=True)
    r = np.log(np.exp(v - m).sum(axis=axis, keepdims=True)) + m
    return r if keepdims else np.squeeze(r, axis=axis)


def setup_inputs():
    t = np.exp2(np.round(np.log2(mx_kscale(D)) / 2))
    return {"x": bf(np.random.standard_normal((B, D)) * 0.1 * t),
            "means": bf(np.random.standard_normal((C * K, D)) * 0.1 * t),
            "bandwidths": bf(0.15 * np.exp(0.2 * np.random.standard_normal((C * K, D))) * t * t),
            "weights": bf(np.random.standard_normal(C * K) * 0.5),
            "priors": bf(np.random.standard_normal(C) * 0.5)}


def reference(x, means, bandwidths, weights, priors):
    x = f64(x)
    means = f64(means)
    b = np.clip(f64(bandwidths), 1e-6, 1000.0)
    w = softmax(f64(weights).reshape(C, K), 1) + 1e-6
    p = softmax(f64(priors), 0) + 1e-6

    inv_b = 1.0 / b
    md = ((mxq(x * x, 1, "e4m3") @ mxq(inv_b, 1, "e4m3").T)
          - 2.0 * (mxq(x, 1, "e4m3") @ mxq(means * inv_b, 1, "e4m3").T)
          + np.sum(means * means * inv_b, axis=1))
    logdet = np.sum(np.log(b), axis=1)
    log_prob = -0.5 * (D * LOG_2PI + logdet + md)

    log_prob = log_prob + np.log(w).reshape(C * K)
    log_prob = logsumexp(log_prob.reshape(-1, C, K), 2)

    log_prob = log_prob + np.log(p)
    log_mixture = log_prob - logsumexp(log_prob, 1, keepdims=True)
    return log_mixture

@@ -1,0 +1,437 @@
+from contextlib import ExitStack
+import math
+
+import concourse.mybir as mybir
+from concourse.masks import make_identity
+
+F32 = mybir.dt.float32
+BF16 = mybir.dt.bfloat16
+U32 = mybir.dt.uint32
+U8 = mybir.dt.uint8
+FP8X4 = mybir.dt.float8_e4m3fn_x4
+ALU = mybir.AluOpType
+ACT = mybir.ActivationFunctionType
+AX = mybir.AxisListType
+
+P = 128
+D = 512
+B = 1024
+NCOMP = 3200
+NCLS = 200
+KC = 16
+NB = B // P
+NT = NCOMP // P
+CT = 4
+NCH = (NT + CT - 1) // CT
+CCH = CT * P // KC
+G8 = P // KC
+LOG_2PI = math.log(2.0 * math.pi)
+UP = 2.0 ** 60
+FLOPS = 2 * 2 * B * NCOMP * D
+
+CLIP_ON_POOL = True
+Q_ON_VECTOR = (0, 1)
+POOL_SUM_PAIRS = ()
+
+
+def tile_dgmmc_diagonal_kernel(tc, x, means, bandwidths, weights, priors, out):
+    nc = tc.nc
+    with ExitStack() as ctx:
+        keep = ctx.enter_context(tc.tile_pool(name="keep", bufs=1))
+        psum = ctx.enter_context(tc.psum_pool(name="psum", bufs=1))
+        ctx.enter_context(tc.manual_schedule())
+
+        def tiles_of(c):
+            return range(c * CT, min(NT, (c + 1) * CT))
+
+        def span(c):
+            ts = tiles_of(c)
+            return slice(ts[0], ts[-1] + 1)
+
+        ident_f = keep.tile([P, P], F32)
+        ident_b = keep.tile([P, P], BF16)
+        m_raw = keep.tile([P, NT, D], BF16)
+        binv = keep.tile([P, NT, D], F32)
+        xc = keep.tile([P, B], U32, align_bytes=64)
+        xs = keep.tile([P, B], U8, align_bytes=64)
+        xxc = keep.tile([P, B], U32, align_bytes=64)
+        xxs = keep.tile([P, B], U8, align_bytes=64)
+        ld = keep.tile([P, NT], F32)
+        s_m = keep.tile([P, NT], F32)
+        lw2t = keep.tile([P, NT], F32)
+        ldw = keep.tile([P, NT], F32)
+        junk = keep.tile([P, D], F32)
+        neg_m = keep.tile([P, NCH, NB], F32)
+        s_sum = keep.tile([P, NCH, NB], F32)
+        s_cls = keep.tile([P, NB, NCH, CCH], F32)
+        res = keep.tile([P, NB, NCLS], F32)
+        eps_t = keep.tile([P, 1], F32)
+        tiny_t = keep.tile([P, 1], F32)
+
+        bw_v = bandwidths.rearrange("(t p) d -> p t d", p=P)
+        m_v = means.rearrange("(t p) d -> p t d", p=P)
+        bw_t = {}
+
+        def load_bw(c):
+            bw_t[c] = keep.tile([P, CT, D], BF16, tag="bw", bufs=3, name="bw")
+            nc.sync.dma_start(out=bw_t[c][:, 0 : len(tiles_of(c)), :], in_=bw_v[:, span(c), :])
+
+        def clip(c, i0, i1):
+            ts = tiles_of(c)
+            i1 = min(i1, len(ts))
+            eng = nc.gpsimd if CLIP_ON_POOL else nc.vector
+            eng.tensor_scalar(
+                out=binv[:, ts[0] + i0 : ts[0] + i1, :],
+                in0=bw_t[c][:, i0:i1, :],
+                scalar1=1000.0,
+                scalar2=1.0e-6,
+                op0=ALU.min,
+                op1=ALU.max,
+            )
+
+        def logs(c):
+            for t in tiles_of(c):
+                nc.scalar.activation(out=binv[:, t, :], in_=binv[:, t, :], func=ACT.Ln, accum_out=ld[:, t : t + 1])
+
+        with tc.tile_pool(name="early", bufs=1) as early:
+            x_raw = early.tile([P, NB, D], BF16)
+            xg = early.tile([P, NB, P, 4], BF16, align_bytes=64)
+            xxg = early.tile([P, NB, P, 4], BF16, align_bytes=64)
+            w_sb = early.tile([P, G8, KC], BF16)
+            w_f = early.tile([P, G8, KC], F32)
+            w_max = early.tile([P, G8], F32)
+            w_sum = early.tile([P, G8], F32)
+            w_rec = early.tile([P, G8], F32)
+            pr_bc = early.tile([P, NCLS], BF16)
+            pr_e = early.tile([P, NCLS], F32)
+            pr_nmax = early.tile([P, 1], F32)
+            pr_sum = early.tile([P, 1], F32)
+            pr_rec = early.tile([P, 1], F32)
+            pr_t = early.tile([P, G8], BF16)
+            pr_tf = early.tile([P, G8], F32)
+            lwp = early.tile([P, G8, KC], F32)
+
+            nc.gpsimd.memset(lwp[:], 0.0)
+            make_identity(nc, ident_b[:])
+            make_identity(nc, ident_f[:])
+            nc.vector.memset(eps_t[:], 1.0e-6)
+            nc.vector.memset(tiny_t[:], 2.0 ** -63)
+
+            nc.scalar.dma_start(out=w_sb[0:NT], in_=weights.rearrange("(t c k) -> t c k", c=G8, k=KC))
+            nc.scalar.dma_start(out=pr_bc[:], in_=priors.partition_broadcast(P))
+            nc.scalar.dma_start(out=pr_t[0:NT], in_=priors.rearrange("(t c) -> t c", c=G8))
+
+            load_bw(0)
+            nc.sync.dma_start(out=x_raw[:], in_=x.rearrange("(n p) d -> p n d", p=P))
+            load_bw(1)
+            load_bw(2)
+
+            R = NT
+            nc.vector.tensor_reduce(out=w_max[0:R], in_=w_sb[0:R], axis=AX.X, op=ALU.max)
+            nc.vector.tensor_tensor(
+                out=w_f[0:R], in0=w_sb[0:R], in1=w_max[0:R].unsqueeze(2).to_broadcast([R, G8, KC]), op=ALU.subtract
+            )
+            nc.vector.tensor_reduce(out=pr_nmax[:], in_=pr_bc[:], axis=AX.X, op=ALU.max, negate=True)
+            nc.scalar.activation(out=w_f[0:R], in_=w_f[0:R], func=ACT.Exp)
+            nc.scalar.activation(out=pr_e[:], in_=pr_bc[:], func=ACT.Exp, bias=pr_nmax[:], accum_out=pr_sum[:])
+            nc.scalar.activation(out=pr_tf[0:R], in_=pr_t[0:R], func=ACT.Exp, bias=pr_nmax[0:R])
+            nc.vector.tensor_reduce(out=w_sum[0:R], in_=w_f[0:R], axis=AX.X, op=ALU.add)
+            nc.vector.reciprocal(out=w_rec[0:R], in_=w_sum[0:R])
+            nc.vector.tensor_tensor(
+                out=w_f[0:R], in0=w_f[0:R], in1=w_rec[0:R].unsqueeze(2).to_broadcast([R, G8, KC]), op=ALU.mult
+            )
+            nc.vector.reciprocal(out=pr_rec[:], in_=pr_sum[:])
+            nc.vector.tensor_scalar(out=pr_tf[0:R], in0=pr_tf[0:R], scalar1=pr_rec[0:R], scalar2=None, op0=ALU.mult)
+
+            for i in range(CT):
+                clip(0, i, i + 1)
+            logs(0)
+            nc.scalar.activation(out=w_f[0:R], in_=w_f[0:R], func=ACT.Ln, bias=eps_t[0:R])
+            nc.scalar.activation(out=pr_tf[0:R], in_=pr_tf[0:R], func=ACT.Ln, bias=eps_t[0:R])
+
+            for n in range(NB):
+                xt = psum.tile([P, 4, P], BF16, tag="tp", bufs=4, name="xt")
+                for t in range(4):
+                    nc.tensor.transpose(xt[:, t, :], x_raw[:, n, t * P : (t + 1) * P], ident_b[:])
+                nc.vector.tensor_scalar(
+                    out=xg[:, n, :, :], in0=xt[:].rearrange("p t r -> p r t"), scalar1=-0.5, scalar2=None, op0=ALU.mult
+                )
+            xg_flat = xg[:].rearrange("p n r t -> p (n r t)")
+            xxg_flat = xxg[:].rearrange("p n r t -> p (n r t)")
+            nc.vector.tensor_tensor(out=xxg_flat, in0=xg_flat, in1=xg_flat, op=ALU.mult)
+            nc.vector.quantize_mx(out=xc[:].bitcast(FP8X4), scales=xs[:], in_=xg_flat)
+            nc.vector.quantize_mx(out=xxc[:].bitcast(FP8X4), scales=xxs[:], in_=xxg_flat)
+
+            nc.vector.tensor_tensor(
+                out=lwp[0:R], in0=w_f[0:R], in1=pr_tf[0:R].unsqueeze(2).to_broadcast([R, G8, KC]), op=ALU.add
+            )
+            lt = psum.tile([P, P], F32, tag="cbp", name="lt")
+            nc.tensor.transpose(lt[:], lwp[:].rearrange("p c k -> p (c k)"), ident_f[:])
+            nc.vector.tensor_scalar(
+                out=lw2t[:], in0=lt[:, 0:NT], scalar1=-0.5 * D * LOG_2PI, scalar2=None, op0=ALU.add
+            )
+
+            for c in range(1, NCH):
+                clip(c, 0, CT)
+                if c + 2 < NCH:
+                    load_bw(c + 2)
+                logs(c)
+            for c in range(NCH):
+                nc.sync.dma_start(out=m_raw[:, span(c), :], in_=m_v[:, span(c), :])
+            nc.gpsimd.memset(s_cls[:], 0.0)
+            nc.vector.scalar_tensor_tensor(
+                out=ldw[:], in0=ld[:], scalar=-0.5, in1=lw2t[:], op0=ALU.mult, op1=ALU.add
+            )
+
+        work = ctx.enter_context(tc.tile_pool(name="work", bufs=2))
+
+        st = {}
+
+        def invert(c):
+            if c < NCH:
+                for t in tiles_of(c):
+                    nc.scalar.activation(out=binv[:, t, :], in_=binv[:, t, :], func=ACT.Exp, scale=-1.0)
+
+        def turn(i, src, dst):
+            tp = psum.tile([P, 4, P], F32, tag="tp", bufs=4, name="tp")
+            for t in range(4):
+                nc.tensor.transpose(tp[:, t, :], src[:, t * P : (t + 1) * P], ident_f[:])
+            nc.scalar.copy(out=dst[:, i * P : (i + 1) * P, :], in_=tp[:].rearrange("p t r -> p r t"))
+
+        def turn_inv(c, i):
+            ts = tiles_of(c)
+            if i == 0:
+                st[("ginv", c)] = work.tile([P, CT * P, 4], BF16, tag="ginv", align_bytes=64, name="ginv")
+            if i < len(ts):
+                turn(i, binv[:, ts[i], :], st[("ginv", c)])
+
+        def make_q(c):
+            if c >= NCH:
+                return
+            ts = tiles_of(c)
+            q = work.tile([P, CT, D], F32, tag="q", bufs=3, name="q")
+            st[("q", c)] = q
+            if c in Q_ON_VECTOR:
+                for i in range(len(ts)):
+                    nc.vector.tensor_tensor(out=q[:, i, :], in0=m_raw[:, ts[i], :], in1=binv[:, ts[i], :], op=ALU.mult)
+            else:
+                nc.gpsimd.tensor_tensor(
+                    out=q[:, 0 : len(ts), :], in0=m_raw[:, span(c), :], in1=binv[:, span(c), :], op=ALU.mult
+                )
+
+        def row_sum(c, i):
+            ts = tiles_of(c)
+            if i < len(ts):
+                t = ts[i]
+                nc.vector.scalar_tensor_tensor(
+                    out=junk[:],
+                    in0=st[("q", c)][:, i, :],
+                    scalar=1.0,
+                    in1=m_raw[:, t, :],
+                    op0=ALU.mult,
+                    op1=ALU.mult,
+                    accum_out=s_m[:, t : t + 1],
+                )
+
+        def turn_q(c, i):
+            ts = tiles_of(c)
+            if i == 0:
+                st[("gq", c)] = work.tile([P, CT * P, 4], BF16, tag="gq", align_bytes=64, name="gq")
+            if i < len(ts):
+                turn(i, st[("q", c)][:, i, :], st[("gq", c)])
+
+        def const_vec(c):
+            cv = work.tile([P, CT], F32, tag="cv", name="cv")
+            st[("cv", c)] = cv
+            nc.vector.scalar_tensor_tensor(
+                out=cv[:, 0 : len(tiles_of(c))],
+                in0=s_m[:, span(c)],
+                scalar=-0.5,
+                in1=ldw[:, span(c)],
+                op0=ALU.mult,
+                op1=ALU.add,
+            )
+
+        def const_spread(c):
+            ts = tiles_of(c)
+            w = len(ts) * P
+            cbp = psum.tile([P, CT * P], F32, tag="cbp", name="cbp")
+            for i in range(len(ts)):
+                nc.tensor.matmul(
+                    out=cbp[:, i * P : (i + 1) * P],
+                    lhsT=st[("cv", c)][:, i : i + 1].to_broadcast([P, P]),
+                    rhs=ident_f[:],
+                    start=True,
+                    stop=True,
+                )
+            cb = work.tile([P, CT * P], F32, tag="cb", name="cb")
+            st[("cb", c)] = cb
+            nc.scalar.copy(out=cb[:, 0:w], in_=cbp[:, 0:w])
+
+        def quantise(c, key):
+            w = len(tiles_of(c)) * P
+            codes = work.tile([P, CT * P], U32, tag=key + "c", align_bytes=64, name=key + "c")
+            scales = work.tile([P, CT * P], U8, tag=key + "s", align_bytes=64, name=key + "s")
+            st[(key + "c", c)] = codes
+            st[(key + "s", c)] = scales
+            nc.vector.quantize_mx(
+                out=codes[:, 0:w].bitcast(FP8X4),
+                scales=scales[:, 0:w],
+                in_=st[(key, c)][:, 0:w, :].rearrange("p r t -> p (r t)"),
+            )
+
+        def mm(c, n):
+            if n >= NB:
+                return
+            w = len(tiles_of(c)) * P
+            cols = slice(n * P, (n + 1) * P)
+            acc = psum.tile([P, CT * P], F32, tag="acc", bufs=3, name="acc")
+            st[("acc", c, n)] = acc
+            nc.tensor.matmul_mx(
+                out=acc[:, 0:w],
+                lhsT=xxc[:, cols].bitcast(FP8X4),
+                lhsT_scale=xxs[:, cols],
+                rhs=st[("ginvc", c)][:, 0:w].bitcast(FP8X4),
+                rhs_scale=st[("ginvs", c)][:, 0:w],
+                start=True,
+                stop=False,
+            )
+            nc.tensor.matmul_mx(
+                out=acc[:, 0:w],
+                lhsT=xc[:, cols].bitcast(FP8X4),
+                lhsT_scale=xs[:, cols],
+                rhs=st[("gqc", c)][:, 0:w].bitcast(FP8X4),
+                rhs_scale=st[("gqs", c)][:, 0:w],
+                start=False,
+                stop=True,
+            )
+
+        def pair(c, k):
+            w = len(tiles_of(c)) * P
+            z2 = work.tile([P, 2, CT * P], F32, tag="z2", bufs=3, name="z2")
+            e2 = work.tile([P, 2, CT * P], F32, tag="e2", bufs=3, name="e2")
+            st[("e2", c, k)] = e2
+            for j in range(2):
+                n = 2 * k + j
+                nc.vector.scalar_tensor_tensor(
+                    out=z2[:, j, 0:w],
+                    in0=st[("acc", c, n)][:, 0:w],
+                    scalar=-2.0,
+                    in1=st[("cb", c)][:, 0:w],
+                    op0=ALU.mult,
+                    op1=ALU.add,
+                )
+                mm(c, n + 3)
+            nc.vector.tensor_reduce(
+                out=neg_m[:, c, 2 * k : 2 * k + 2], in_=z2[:, :, 0:w], axis=AX.X, op=ALU.max, negate=True
+            )
+            for j in range(2):
+                n = 2 * k + j
+                nc.scalar.activation(
+                    out=e2[:, j, 0:w], in_=z2[:, j, 0:w], func=ACT.Exp, bias=neg_m[:, c, n : n + 1]
+                )
+
+        def class_sum(c, k):
+            w = len(tiles_of(c)) * P
+            nc.vector.tensor_reduce(
+                out=s_cls[:, 2 * k : 2 * k + 2, c, 0 : w // KC],
+                in_=st[("e2", c, k)][:, :, 0:w].rearrange("p j (c k) -> p j c k", k=KC),
+                axis=AX.X,
+                op=ALU.add,
+            )
+
+        def chunk_sum(c):
+            nc.vector.tensor_reduce(out=s_sum[:, c, :], in_=s_cls[:, :, c, :], axis=AX.X, op=ALU.add)
+
+        invert(0)
+        make_q(0)
+        for c in range(-1, NCH):
+            p = c + 1
+            has_main = c >= 0
+            has_prep = p < NCH
+            if has_prep:
+                for i in range(CT):
+                    turn_inv(p, i)
+            if c == -1:
+                invert(1)
+            else:
+                make_q(c + 2)
+            if has_main:
+                for n in range(3):
+                    mm(c, n)
+            if has_prep:
+                for i in range(CT):
+                    row_sum(p, i)
+                const_vec(p)
+                const_spread(p)
+            if has_main:
+                pair(c, 0)
+            if has_prep:
+                turn_q(p, 0)
+            if has_main:
+                pair(c, 1)
+            if has_prep:
+                turn_q(p, 1)
+            if has_main:
+                class_sum(c, 0)
+                pair(c, 2)
+            if has_prep:
+                turn_q(p, 2)
+                turn_q(p, 3)
+            if has_main:
+                class_sum(c, 1)
+                pair(c, 3)
+            if has_prep:
+                quantise(p, "ginv")
+                quantise(p, "gq")
+            if c == -1:
+                make_q(1)
+            if has_main:
+                class_sum(c, 2)
+                class_sum(c, 3)
+                chunk_sum(c)
+            invert(c + 3)
+
+        g_min = keep.tile([P, NB], F32)
+        dd = keep.tile([P, NCH, NB], F32)
+        ft = keep.tile([P, NCH, NB], F32)
+        tot = keep.tile([P, NB], F32)
+        rec = keep.tile([P, NB], F32)
+        gg = keep.tile([P, NB, NCH], F32)
+        nc.vector.tensor_reduce(out=g_min[:], in_=neg_m[:].rearrange("p c n -> p n c"), axis=AX.X, op=ALU.min)
+        nc.vector.tensor_tensor(
+            out=dd[:], in0=g_min[:].unsqueeze(1).to_broadcast([P, NCH, NB]), in1=neg_m[:], op=ALU.subtract
+        )
+        nc.scalar.activation(out=dd[:], in_=dd[:], func=ACT.Exp)
+        nc.vector.tensor_tensor(out=ft[:], in0=dd[:], in1=s_sum[:], op=ALU.mult)
+        nc.vector.tensor_reduce(out=tot[:], in_=ft[:].rearrange("p c n -> p n c"), axis=AX.X, op=ALU.add)
+        nc.vector.reciprocal(out=rec[:], in_=tot[:])
+        nc.vector.scalar_tensor_tensor(
+            out=gg[:].rearrange("p n c -> p c n"),
+            in0=dd[:],
+            scalar=UP,
+            in1=rec[:].unsqueeze(1).to_broadcast([P, NCH, NB]),
+            op0=ALU.mult,
+            op1=ALU.mult,
+        )
+        out_v = out.rearrange("(n p) c -> p n c", p=P)
+        H = NB // 2
+        for h in range(2):
+            ns = slice(h * H, (h + 1) * H)
+            sv = s_cls[:, ns, :, :].rearrange("p n c k -> p (n c) k")
+            nc.vector.tensor_tensor(
+                out=sv,
+                in0=sv,
+                in1=gg[:, ns, :].rearrange("p n c -> p (n c)").unsqueeze(2).to_broadcast([P, H * NCH, CCH]),
+                op=ALU.mult,
+            )
+            nc.scalar.activation(
+                out=res[:, ns, :],
+                in_=s_cls[:, ns, :, :].rearrange("p n c k -> p n (c k)")[:, :, 0:NCLS],
+                func=ACT.Ln,
+                bias=tiny_t[:],
+            )
+            nc.vector.tensor_scalar(
+                out=res[:, ns, :], in0=res[:, ns, :], scalar1=-60.0 * math.log(2.0), scalar2=None, op0=ALU.add
+            )
+            nc.sync.dma_start(out=out_v[:, ns, :], in_=res[:, ns, :])

@@ -29,9 +29,10 @@ LOG_2PI = math.log(2.0 * math.pi)
 UP = 2.0 ** 60
 FLOPS = 2 * 2 * B * NCOMP * D
 
-CLIP_ON_POOL = True
+CLIP_ON_POOL = False
 Q_ON_VECTOR = (0, 1)
-POOL_SUM_PAIRS = ()
+POOL_SUM = (0, 1)
+QN = 4
 
 
 def tile_dgmmc_diagonal_kernel(tc, x, means, bandwidths, weights, priors, out):
@@ -122,8 +123,8 @@ def tile_dgmmc_diagonal_kernel(tc, x, means, bandwidths, weights, priors, out):
             nc.scalar.dma_start(out=pr_t[0:NT], in_=priors.rearrange("(t c) -> t c", c=G8))
 
             load_bw(0)
-            nc.sync.dma_start(out=x_raw[:], in_=x.rearrange("(n p) d -> p n d", p=P))
             load_bw(1)
+            nc.sync.dma_start(out=x_raw[:], in_=x.rearrange("(n p) d -> p n d", p=P))
             load_bw(2)
 
             R = NT
@@ -135,6 +136,9 @@ def tile_dgmmc_diagonal_kernel(tc, x, means, bandwidths, weights, priors, out):
             nc.scalar.activation(out=w_f[0:R], in_=w_f[0:R], func=ACT.Exp)
             nc.scalar.activation(out=pr_e[:], in_=pr_bc[:], func=ACT.Exp, bias=pr_nmax[:], accum_out=pr_sum[:])
             nc.scalar.activation(out=pr_tf[0:R], in_=pr_t[0:R], func=ACT.Exp, bias=pr_nmax[0:R])
+            for i in range(CT):
+                clip(0, i, i + 1)
+            logs(0)
             nc.vector.tensor_reduce(out=w_sum[0:R], in_=w_f[0:R], axis=AX.X, op=ALU.add)
             nc.vector.reciprocal(out=w_rec[0:R], in_=w_sum[0:R])
             nc.vector.tensor_tensor(
@@ -143,41 +147,48 @@ def tile_dgmmc_diagonal_kernel(tc, x, means, bandwidths, weights, priors, out):
             nc.vector.reciprocal(out=pr_rec[:], in_=pr_sum[:])
             nc.vector.tensor_scalar(out=pr_tf[0:R], in0=pr_tf[0:R], scalar1=pr_rec[0:R], scalar2=None, op0=ALU.mult)
 
-            for i in range(CT):
-                clip(0, i, i + 1)
-            logs(0)
             nc.scalar.activation(out=w_f[0:R], in_=w_f[0:R], func=ACT.Ln, bias=eps_t[0:R])
             nc.scalar.activation(out=pr_tf[0:R], in_=pr_tf[0:R], func=ACT.Ln, bias=eps_t[0:R])
 
-            for n in range(NB):
+            def next_logs(c):
+                clip(c, 0, CT)
+                if c + 2 < NCH:
+                    load_bw(c + 2)
+                logs(c)
+
+            def x_turn(n):
                 xt = psum.tile([P, 4, P], BF16, tag="tp", bufs=4, name="xt")
                 for t in range(4):
                     nc.tensor.transpose(xt[:, t, :], x_raw[:, n, t * P : (t + 1) * P], ident_b[:])
                 nc.vector.tensor_scalar(
                     out=xg[:, n, :, :], in0=xt[:].rearrange("p t r -> p r t"), scalar1=-0.5, scalar2=None, op0=ALU.mult
                 )
+
             xg_flat = xg[:].rearrange("p n r t -> p (n r t)")
             xxg_flat = xxg[:].rearrange("p n r t -> p (n r t)")
+            next_logs(1)
+            next_logs(2)
+            for n in range(0, 4):
+                x_turn(n)
+            next_logs(3)
+            for n in range(4, 8):
+                x_turn(n)
+            next_logs(4)
+            next_logs(5)
+            for c in range(NCH):
+                nc.sync.dma_start(out=m_raw[:, span(c), :], in_=m_v[:, span(c), :])
             nc.vector.tensor_tensor(out=xxg_flat, in0=xg_flat, in1=xg_flat, op=ALU.mult)
+            next_logs(6)
             nc.vector.quantize_mx(out=xc[:].bitcast(FP8X4), scales=xs[:], in_=xg_flat)
-            nc.vector.quantize_mx(out=xxc[:].bitcast(FP8X4), scales=xxs[:], in_=xxg_flat)
-
             nc.vector.tensor_tensor(
                 out=lwp[0:R], in0=w_f[0:R], in1=pr_tf[0:R].unsqueeze(2).to_broadcast([R, G8, KC]), op=ALU.add
             )
             lt = psum.tile([P, P], F32, tag="cbp", name="lt")
             nc.tensor.transpose(lt[:], lwp[:].rearrange("p c k -> p (c k)"), ident_f[:])
+            nc.vector.quantize_mx(out=xxc[:].bitcast(FP8X4), scales=xxs[:], in_=xxg_flat)
             nc.vector.tensor_scalar(
                 out=lw2t[:], in0=lt[:, 0:NT], scalar1=-0.5 * D * LOG_2PI, scalar2=None, op0=ALU.add
             )
-
-            for c in range(1, NCH):
-                clip(c, 0, CT)
-                if c + 2 < NCH:
-                    load_bw(c + 2)
-                logs(c)
-            for c in range(NCH):
-                nc.sync.dma_start(out=m_raw[:, span(c), :], in_=m_v[:, span(c), :])
             nc.gpsimd.memset(s_cls[:], 0.0)
             nc.vector.scalar_tensor_tensor(
                 out=ldw[:], in0=ld[:], scalar=-0.5, in1=lw2t[:], op0=ALU.mult, op1=ALU.add
@@ -188,9 +199,11 @@ def tile_dgmmc_diagonal_kernel(tc, x, means, bandwidths, weights, priors, out):
         st = {}
 
         def invert(c):
-            if c < NCH:
+            if c < 2:
                 for t in tiles_of(c):
                     nc.scalar.activation(out=binv[:, t, :], in_=binv[:, t, :], func=ACT.Exp, scale=-1.0)
+            elif c < NCH:
+                nc.scalar.activation(out=binv[:, span(c), :], in_=binv[:, span(c), :], func=ACT.Exp, scale=-1.0)
 
         def turn(i, src, dst):
             tp = psum.tile([P, 4, P], F32, tag="tp", bufs=4, name="tp")
@@ -306,15 +319,14 @@ def tile_dgmmc_diagonal_kernel(tc, x, means, bandwidths, weights, priors, out):
                 stop=True,
             )
 
-        def pair(c, k):
+        def adds(c, h):
             w = len(tiles_of(c)) * P
-            z2 = work.tile([P, 2, CT * P], F32, tag="z2", bufs=3, name="z2")
-            e2 = work.tile([P, 2, CT * P], F32, tag="e2", bufs=3, name="e2")
-            st[("e2", c, k)] = e2
-            for j in range(2):
-                n = 2 * k + j
+            z4 = work.tile([P, QN, CT * P], F32, tag="z4", bufs=2, name="z4")
+            st[("z4", c, h)] = z4
+            for j in range(QN):
+                n = QN * h + j
                 nc.vector.scalar_tensor_tensor(
-                    out=z2[:, j, 0:w],
+                    out=z4[:, j, 0:w],
                     in0=st[("acc", c, n)][:, 0:w],
                     scalar=-2.0,
                     in1=st[("cb", c)][:, 0:w],
@@ -322,23 +334,33 @@ def tile_dgmmc_diagonal_kernel(tc, x, means, bandwidths, weights, priors, out):
                     op1=ALU.add,
                 )
                 mm(c, n + 3)
+
+        def zmax(c, h):
+            w = len(tiles_of(c)) * P
+            z4 = st[("z4", c, h)]
+            e4 = work.tile([P, QN, CT * P], F32, tag="e4", bufs=3, name="e4")
+            st[("e4", c, h)] = e4
             nc.vector.tensor_reduce(
-                out=neg_m[:, c, 2 * k : 2 * k + 2], in_=z2[:, :, 0:w], axis=AX.X, op=ALU.max, negate=True
+                out=neg_m[:, c, QN * h : QN * (h + 1)], in_=z4[:, :, 0:w], axis=AX.X, op=ALU.max, negate=True
             )
-            for j in range(2):
-                n = 2 * k + j
+            for j in range(QN):
+                n = QN * h + j
                 nc.scalar.activation(
-                    out=e2[:, j, 0:w], in_=z2[:, j, 0:w], func=ACT.Exp, bias=neg_m[:, c, n : n + 1]
+                    out=e4[:, j, 0:w], in_=z4[:, j, 0:w], func=ACT.Exp, bias=neg_m[:, c, n : n + 1]
                 )
 
-        def class_sum(c, k):
+        def class_sum(c, h):
             w = len(tiles_of(c)) * P
-            nc.vector.tensor_reduce(
-                out=s_cls[:, 2 * k : 2 * k + 2, c, 0 : w // KC],
-                in_=st[("e2", c, k)][:, :, 0:w].rearrange("p j (c k) -> p j c k", k=KC),
-                axis=AX.X,
-                op=ALU.add,
-            )
+            ev = st[("e4", c, h)][:, :, 0:w].rearrange("p j (c k) -> p j c k", k=KC)
+            dst = s_cls[:, QN * h : QN * (h + 1), c, 0 : w // KC]
+            if h in POOL_SUM:
+                for half in (8, 4, 2):
+                    nc.gpsimd.tensor_tensor(
+                        out=ev[:, :, :, 0:half], in0=ev[:, :, :, 0:half], in1=ev[:, :, :, half : 2 * half], op=ALU.add
+                    )
+                nc.gpsimd.tensor_tensor(out=dst, in0=ev[:, :, :, 0], in1=ev[:, :, :, 1], op=ALU.add)
+            else:
+                nc.vector.tensor_reduce(out=dst, in_=ev, axis=AX.X, op=ALU.add)
 
         def chunk_sum(c):
             nc.vector.tensor_reduce(out=s_sum[:, c, :], in_=s_cls[:, :, c, :], axis=AX.X, op=ALU.add)
@@ -349,49 +371,46 @@ def tile_dgmmc_diagonal_kernel(tc, x, means, bandwidths, weights, priors, out):
             p = c + 1
             has_main = c >= 0
             has_prep = p < NCH
-            if has_prep:
-                for i in range(CT):
-                    turn_inv(p, i)
+
+            def prep(f, *args):
+                if has_prep:
+                    f(p, *args)
+
+            def main(f, *args):
+                if has_main:
+                    f(c, *args)
+
+            for i in range(CT):
+                prep(turn_inv, i)
             if c == -1:
                 invert(1)
             else:
                 make_q(c + 2)
-            if has_main:
-                for n in range(3):
-                    mm(c, n)
-            if has_prep:
-                for i in range(CT):
-                    row_sum(p, i)
-                const_vec(p)
-                const_spread(p)
-            if has_main:
-                pair(c, 0)
-            if has_prep:
-                turn_q(p, 0)
-            if has_main:
-                pair(c, 1)
-            if has_prep:
-                turn_q(p, 1)
-            if has_main:
-                class_sum(c, 0)
-                pair(c, 2)
-            if has_prep:
-                turn_q(p, 2)
-                turn_q(p, 3)
-            if has_main:
-                class_sum(c, 1)
-                pair(c, 3)
-            if has_prep:
-                quantise(p, "ginv")
-                quantise(p, "gq")
+            for n in range(3):
+                main(mm, n)
+            main(adds, 0)
+            prep(row_sum, 0)
+            prep(row_sum, 1)
+            main(zmax, 0)
+            for i in range(CT):
+                prep(turn_q, i)
+            main(adds, 1)
+            prep(row_sum, 2)
+            prep(row_sum, 3)
+            prep(const_vec)
+            main(zmax, 1)
+            prep(const_spread)
+            main(class_sum, 0)
+            prep(quantise, "ginv")
+            prep(quantise, "gq")
             if c == -1:
                 make_q(1)
-            if has_main:
-                class_sum(c, 2)
-                class_sum(c, 3)
-                chunk_sum(c)
+            main(class_sum, 1)
+            if c >= 1:
+                chunk_sum(c - 1)
             invert(c + 3)
 
+        chunk_sum(NCH - 1)
         g_min = keep.tile([P, NB], F32)
         dd = keep.tile([P, NCH, NB], F32)
         ft = keep.tile([P, NCH, NB], F32)

@@ -31,7 +31,7 @@ FLOPS = 2 * 2 * B * NCOMP * D
 
 CLIP_ON_POOL = False
 Q_ON_VECTOR = (0, 1)
-POOL_SUM = (0, 1)
+POOL_SUM = ()
 QN = 4
 
 
@@ -199,11 +199,9 @@ def tile_dgmmc_diagonal_kernel(tc, x, means, bandwidths, weights, priors, out):
         st = {}
 
         def invert(c):
-            if c < 2:
+            if c < NCH:
                 for t in tiles_of(c):
                     nc.scalar.activation(out=binv[:, t, :], in_=binv[:, t, :], func=ACT.Exp, scale=-1.0)
-            elif c < NCH:
-                nc.scalar.activation(out=binv[:, span(c), :], in_=binv[:, span(c), :], func=ACT.Exp, scale=-1.0)
 
         def turn(i, src, dst):
             tp = psum.tile([P, 4, P], F32, tag="tp", bufs=4, name="tp")
@@ -406,11 +404,9 @@ def tile_dgmmc_diagonal_kernel(tc, x, means, bandwidths, weights, priors, out):
             if c == -1:
                 make_q(1)
             main(class_sum, 1)
-            if c >= 1:
-                chunk_sum(c - 1)
+            main(chunk_sum)
             invert(c + 3)
 
-        chunk_sum(NCH - 1)
         g_min = keep.tile([P, NB], F32)
         dd = keep.tile([P, NCH, NB], F32)
         ft = keep.tile([P, NCH, NB], F32)

@@ -31,7 +31,6 @@ FLOPS = 2 * 2 * B * NCOMP * D
 
 CLIP_ON_POOL = False
 Q_ON_VECTOR = (0, 1)
-POOL_SUM = ()
 QN = 4
 
 
@@ -51,6 +50,7 @@ def tile_dgmmc_diagonal_kernel(tc, x, means, bandwidths, weights, priors, out):
 
         ident_f = keep.tile([P, P], F32)
         ident_b = keep.tile([P, P], BF16)
+        perm_f = keep.tile([P, P], F32)
         m_raw = keep.tile([P, NT, D], BF16)
         binv = keep.tile([P, NT, D], F32)
         xc = keep.tile([P, B], U32, align_bytes=64)
@@ -115,6 +115,10 @@ def tile_dgmmc_diagonal_kernel(tc, x, means, bandwidths, weights, priors, out):
             nc.gpsimd.memset(lwp[:], 0.0)
             make_identity(nc, ident_b[:])
             make_identity(nc, ident_f[:])
+            nc.vector.tensor_copy(
+                out=perm_f[:].rearrange("p (h c l) -> p h c l", h=4, c=G8, l=4),
+                in_=ident_f[:].rearrange("p (c h l) -> p h c l", h=4, c=G8, l=4),
+            )
             nc.vector.memset(eps_t[:], 1.0e-6)
             nc.vector.memset(tiny_t[:], 2.0 ** -63)
 
@@ -199,22 +203,28 @@ def tile_dgmmc_diagonal_kernel(tc, x, means, bandwidths, weights, priors, out):
         st = {}
 
         def invert(c):
-            if c < NCH:
+            if c < 2:
                 for t in tiles_of(c):
                     nc.scalar.activation(out=binv[:, t, :], in_=binv[:, t, :], func=ACT.Exp, scale=-1.0)
+            elif c < NCH:
+                nc.scalar.activation(out=binv[:, span(c), :], in_=binv[:, span(c), :], func=ACT.Exp, scale=-1.0)
 
-        def turn(i, src, dst):
+        def turn(c, i, src, dst):
+            w = len(tiles_of(c)) * P
             tp = psum.tile([P, 4, P], F32, tag="tp", bufs=4, name="tp")
             for t in range(4):
-                nc.tensor.transpose(tp[:, t, :], src[:, t * P : (t + 1) * P], ident_f[:])
-            nc.scalar.copy(out=dst[:, i * P : (i + 1) * P, :], in_=tp[:].rearrange("p t r -> p r t"))
+                nc.tensor.transpose(tp[:, t, :], src[:, t * P : (t + 1) * P], perm_f[:])
+            nc.scalar.copy(
+                out=dst[:, 0:w, :].rearrange("p (h m) t -> p h m t", h=4)[:, :, 32 * i : 32 * (i + 1), :],
+                in_=tp[:].rearrange("p t (h m) -> p h m t", h=4),
+            )
 
         def turn_inv(c, i):
             ts = tiles_of(c)
             if i == 0:
                 st[("ginv", c)] = work.tile([P, CT * P, 4], BF16, tag="ginv", align_bytes=64, name="ginv")
             if i < len(ts):
-                turn(i, binv[:, ts[i], :], st[("ginv", c)])
+                turn(c, i, binv[:, ts[i], :], st[("ginv", c)])
 
         def make_q(c):
             if c >= NCH:
@@ -249,7 +259,7 @@ def tile_dgmmc_diagonal_kernel(tc, x, means, bandwidths, weights, priors, out):
             if i == 0:
                 st[("gq", c)] = work.tile([P, CT * P, 4], BF16, tag="gq", align_bytes=64, name="gq")
             if i < len(ts):
-                turn(i, st[("q", c)][:, i, :], st[("gq", c)])
+                turn(c, i, st[("q", c)][:, i, :], st[("gq", c)])
 
         def const_vec(c):
             cv = work.tile([P, CT], F32, tag="cv", name="cv")
@@ -271,13 +281,16 @@ def tile_dgmmc_diagonal_kernel(tc, x, means, bandwidths, weights, priors, out):
                 nc.tensor.matmul(
                     out=cbp[:, i * P : (i + 1) * P],
                     lhsT=st[("cv", c)][:, i : i + 1].to_broadcast([P, P]),
-                    rhs=ident_f[:],
+                    rhs=perm_f[:],
                     start=True,
                     stop=True,
                 )
             cb = work.tile([P, CT * P], F32, tag="cb", name="cb")
             st[("cb", c)] = cb
-            nc.scalar.copy(out=cb[:, 0:w], in_=cbp[:, 0:w])
+            nc.scalar.copy(
+                out=cb[:, 0:w].rearrange("p (h i m) -> p i h m", h=4, i=len(ts)),
+                in_=cbp[:, 0:w].rearrange("p (i h m) -> p i h m", h=4, i=len(ts)),
+            )
 
         def quantise(c, key):
             w = len(tiles_of(c)) * P
@@ -347,18 +360,22 @@ def tile_dgmmc_diagonal_kernel(tc, x, means, bandwidths, weights, priors, out):
                     out=e4[:, j, 0:w], in_=z4[:, j, 0:w], func=ACT.Exp, bias=neg_m[:, c, n : n + 1]
                 )
 
+        def fold(c, h):
+            w = len(tiles_of(c)) * P
+            e4 = st[("e4", c, h)]
+            for half in (w // 2, w // 4):
+                nc.gpsimd.tensor_tensor(
+                    out=e4[:, :, 0:half], in0=e4[:, :, 0:half], in1=e4[:, :, half : 2 * half], op=ALU.add
+                )
+
         def class_sum(c, h):
             w = len(tiles_of(c)) * P
-            ev = st[("e4", c, h)][:, :, 0:w].rearrange("p j (c k) -> p j c k", k=KC)
-            dst = s_cls[:, QN * h : QN * (h + 1), c, 0 : w // KC]
-            if h in POOL_SUM:
-                for half in (8, 4, 2):
-                    nc.gpsimd.tensor_tensor(
-                        out=ev[:, :, :, 0:half], in0=ev[:, :, :, 0:half], in1=ev[:, :, :, half : 2 * half], op=ALU.add
-                    )
-                nc.gpsimd.tensor_tensor(out=dst, in0=ev[:, :, :, 0], in1=ev[:, :, :, 1], op=ALU.add)
-            else:
-                nc.vector.tensor_reduce(out=dst, in_=ev, axis=AX.X, op=ALU.add)
+            nc.vector.tensor_reduce(
+                out=s_cls[:, QN * h : QN * (h + 1), c, 0 : w // KC],
+                in_=st[("e4", c, h)][:, :, 0 : w // 4].rearrange("p j (c l) -> p j c l", l=4),
+                axis=AX.X,
+                op=ALU.add,
+            )
 
         def chunk_sum(c):
             nc.vector.tensor_reduce(out=s_sum[:, c, :], in_=s_cls[:, :, c, :], axis=AX.X, op=ALU.add)
@@ -390,6 +407,7 @@ def tile_dgmmc_diagonal_kernel(tc, x, means, bandwidths, weights, priors, out):
             prep(row_sum, 0)
             prep(row_sum, 1)
             main(zmax, 0)
+            main(fold, 0)
             for i in range(CT):
                 prep(turn_q, i)
             main(adds, 1)
@@ -397,16 +415,20 @@ def tile_dgmmc_diagonal_kernel(tc, x, means, bandwidths, weights, priors, out):
             prep(row_sum, 3)
             prep(const_vec)
             main(zmax, 1)
+            main(fold, 1)
             prep(const_spread)
-            main(class_sum, 0)
+            if c >= 1:
+                class_sum(c - 1, 1)
+                chunk_sum(c - 1)
             prep(quantise, "ginv")
             prep(quantise, "gq")
             if c == -1:
                 make_q(1)
-            main(class_sum, 1)
-            main(chunk_sum)
+            main(class_sum, 0)
             invert(c + 3)
 
+        class_sum(NCH - 1, 1)
+        chunk_sum(NCH - 1)
         g_min = keep.tile([P, NB], F32)
         dd = keep.tile([P, NCH, NB], F32)
         ft = keep.tile([P, NCH, NB], F32)

@@ -30,8 +30,8 @@ UP = 2.0 ** 60
 FLOPS = 2 * 2 * B * NCOMP * D
 
 CLIP_ON_POOL = False
-Q_ON_VECTOR = (0, 1)
 QN = 4
+NU = 2 * NCH
 
 
 def tile_dgmmc_diagonal_kernel(tc, x, means, bandwidths, weights, priors, out):
@@ -50,7 +50,6 @@ def tile_dgmmc_diagonal_kernel(tc, x, means, bandwidths, weights, priors, out):
 
         ident_f = keep.tile([P, P], F32)
         ident_b = keep.tile([P, P], BF16)
-        perm_f = keep.tile([P, P], F32)
         m_raw = keep.tile([P, NT, D], BF16)
         binv = keep.tile([P, NT, D], F32)
         xc = keep.tile([P, B], U32, align_bytes=64)
@@ -115,10 +114,6 @@ def tile_dgmmc_diagonal_kernel(tc, x, means, bandwidths, weights, priors, out):
             nc.gpsimd.memset(lwp[:], 0.0)
             make_identity(nc, ident_b[:])
             make_identity(nc, ident_f[:])
-            nc.vector.tensor_copy(
-                out=perm_f[:].rearrange("p (h c l) -> p h c l", h=4, c=G8, l=4),
-                in_=ident_f[:].rearrange("p (c h l) -> p h c l", h=4, c=G8, l=4),
-            )
             nc.vector.memset(eps_t[:], 1.0e-6)
             nc.vector.memset(tiny_t[:], 2.0 ** -63)
 
@@ -161,7 +156,7 @@ def tile_dgmmc_diagonal_kernel(tc, x, means, bandwidths, weights, priors, out):
                 logs(c)
 
             def x_turn(n):
-                xt = psum.tile([P, 4, P], BF16, tag="tp", bufs=4, name="xt")
+                xt = psum.tile([P, 4, P], BF16, tag="tp", bufs=2, name="xt")
                 for t in range(4):
                     nc.tensor.transpose(xt[:, t, :], x_raw[:, n, t * P : (t + 1) * P], ident_b[:])
                 nc.vector.tensor_scalar(
@@ -187,7 +182,7 @@ def tile_dgmmc_diagonal_kernel(tc, x, means, bandwidths, weights, priors, out):
             nc.vector.tensor_tensor(
                 out=lwp[0:R], in0=w_f[0:R], in1=pr_tf[0:R].unsqueeze(2).to_broadcast([R, G8, KC]), op=ALU.add
             )
-            lt = psum.tile([P, P], F32, tag="cbp", name="lt")
+            lt = psum.tile([P, P], F32, tag="tp", bufs=2, name="lt")
             nc.tensor.transpose(lt[:], lwp[:].rearrange("p c k -> p (c k)"), ident_f[:])
             nc.vector.quantize_mx(out=xxc[:].bitcast(FP8X4), scales=xxs[:], in_=xxg_flat)
             nc.vector.tensor_scalar(
@@ -201,95 +196,68 @@ def tile_dgmmc_diagonal_kernel(tc, x, means, bandwidths, weights, priors, out):
         work = ctx.enter_context(tc.tile_pool(name="work", bufs=2))
 
         st = {}
+        st["pending"] = []
+
+        def flush():
+            for f in st["pending"]:
+                f()
+            st["pending"] = []
 
         def invert(c):
-            if c < 2:
-                for t in tiles_of(c):
-                    nc.scalar.activation(out=binv[:, t, :], in_=binv[:, t, :], func=ACT.Exp, scale=-1.0)
-            elif c < NCH:
+            if 0 <= c < NCH:
                 nc.scalar.activation(out=binv[:, span(c), :], in_=binv[:, span(c), :], func=ACT.Exp, scale=-1.0)
 
-        def turn(c, i, src, dst):
-            w = len(tiles_of(c)) * P
-            tp = psum.tile([P, 4, P], F32, tag="tp", bufs=4, name="tp")
+        def turn(i, src, dst, late):
+            tp = psum.tile([P, 4, P], F32, tag="tp", bufs=2, name="tp")
             for t in range(4):
-                nc.tensor.transpose(tp[:, t, :], src[:, t * P : (t + 1) * P], perm_f[:])
-            nc.scalar.copy(
-                out=dst[:, 0:w, :].rearrange("p (h m) t -> p h m t", h=4)[:, :, 32 * i : 32 * (i + 1), :],
-                in_=tp[:].rearrange("p t (h m) -> p h m t", h=4),
-            )
+                nc.tensor.transpose(tp[:, t, :], src[:, t * P : (t + 1) * P], ident_f[:])
+
+            def evac():
+                nc.scalar.copy(out=dst[:, i * P : (i + 1) * P, :], in_=tp[:].rearrange("p t r -> p r t"))
+
+            if late:
+                st["pending"].append(evac)
+            else:
+                evac()
 
         def turn_inv(c, i):
             ts = tiles_of(c)
             if i == 0:
                 st[("ginv", c)] = work.tile([P, CT * P, 4], BF16, tag="ginv", align_bytes=64, name="ginv")
             if i < len(ts):
-                turn(c, i, binv[:, ts[i], :], st[("ginv", c)])
-
-        def make_q(c):
-            if c >= NCH:
-                return
-            ts = tiles_of(c)
-            q = work.tile([P, CT, D], F32, tag="q", bufs=3, name="q")
-            st[("q", c)] = q
-            if c in Q_ON_VECTOR:
-                for i in range(len(ts)):
-                    nc.vector.tensor_tensor(out=q[:, i, :], in0=m_raw[:, ts[i], :], in1=binv[:, ts[i], :], op=ALU.mult)
-            else:
-                nc.gpsimd.tensor_tensor(
-                    out=q[:, 0 : len(ts), :], in0=m_raw[:, span(c), :], in1=binv[:, span(c), :], op=ALU.mult
-                )
-
-        def row_sum(c, i):
-            ts = tiles_of(c)
-            if i < len(ts):
-                t = ts[i]
-                nc.vector.scalar_tensor_tensor(
-                    out=junk[:],
-                    in0=st[("q", c)][:, i, :],
-                    scalar=1.0,
-                    in1=m_raw[:, t, :],
-                    op0=ALU.mult,
-                    op1=ALU.mult,
-                    accum_out=s_m[:, t : t + 1],
-                )
+                turn(i, binv[:, ts[i], :], st[("ginv", c)], i >= 2)
 
         def turn_q(c, i):
             ts = tiles_of(c)
             if i == 0:
                 st[("gq", c)] = work.tile([P, CT * P, 4], BF16, tag="gq", align_bytes=64, name="gq")
             if i < len(ts):
-                turn(c, i, st[("q", c)][:, i, :], st[("gq", c)])
+                turn(i, st[("q", c)][:, i, :], st[("gq", c)], i >= 2)
 
-        def const_vec(c):
+        def make_q(c):
+            ts = tiles_of(c)
+            q = work.tile([P, CT, D], F32, tag="q", name="q")
+            st[("q", c)] = q
+            nc.vector.tensor_tensor(
+                out=q[:, 0 : len(ts), :], in0=m_raw[:, span(c), :], in1=binv[:, span(c), :], op=ALU.mult
+            )
+
+        def row_sums(c):
+            ts = tiles_of(c)
+            for i in range(len(ts)):
+                nc.vector.scalar_tensor_tensor(
+                    out=junk[:],
+                    in0=st[("q", c)][:, i, :],
+                    scalar=1.0,
+                    in1=m_raw[:, ts[i], :],
+                    op0=ALU.mult,
+                    op1=ALU.mult,
+                    accum_out=s_m[:, ts[i] : ts[i] + 1],
+                )
             cv = work.tile([P, CT], F32, tag="cv", name="cv")
             st[("cv", c)] = cv
             nc.vector.scalar_tensor_tensor(
-                out=cv[:, 0 : len(tiles_of(c))],
-                in0=s_m[:, span(c)],
-                scalar=-0.5,
-                in1=ldw[:, span(c)],
-                op0=ALU.mult,
-                op1=ALU.add,
-            )
-
-        def const_spread(c):
-            ts = tiles_of(c)
-            w = len(ts) * P
-            cbp = psum.tile([P, CT * P], F32, tag="cbp", name="cbp")
-            for i in range(len(ts)):
-                nc.tensor.matmul(
-                    out=cbp[:, i * P : (i + 1) * P],
-                    lhsT=st[("cv", c)][:, i : i + 1].to_broadcast([P, P]),
-                    rhs=perm_f[:],
-                    start=True,
-                    stop=True,
-                )
-            cb = work.tile([P, CT * P], F32, tag="cb", name="cb")
-            st[("cb", c)] = cb
-            nc.scalar.copy(
-                out=cb[:, 0:w].rearrange("p (h i m) -> p i h m", h=4, i=len(ts)),
-                in_=cbp[:, 0:w].rearrange("p (i h m) -> p i h m", h=4, i=len(ts)),
+                out=cv[:, 0 : len(ts)], in0=s_m[:, span(c)], scalar=-0.5, in1=ldw[:, span(c)], op0=ALU.mult, op1=ALU.add
             )
 
         def quantise(c, key):
@@ -304,131 +272,99 @@ def tile_dgmmc_diagonal_kernel(tc, x, means, bandwidths, weights, priors, out):
                 in_=st[(key, c)][:, 0:w, :].rearrange("p r t -> p (r t)"),
             )
 
-        def mm(c, n):
-            if n >= NB:
+        def products(u, i):
+            c, h = divmod(u, 2)
+            if i >= len(tiles_of(c)):
                 return
-            w = len(tiles_of(c)) * P
-            cols = slice(n * P, (n + 1) * P)
-            acc = psum.tile([P, CT * P], F32, tag="acc", bufs=3, name="acc")
-            st[("acc", c, n)] = acc
+            if i == 0:
+                st[("zt", u)] = work.tile([P, CT, QN * P], F32, tag="zt", name="zt")
+            rows = slice(h * QN * P, (h + 1) * QN * P)
+            cols = slice(i * P, (i + 1) * P)
+            acc = psum.tile([P, QN * P], F32, tag="acc", bufs=2, name="acc")
             nc.tensor.matmul_mx(
-                out=acc[:, 0:w],
-                lhsT=xxc[:, cols].bitcast(FP8X4),
-                lhsT_scale=xxs[:, cols],
-                rhs=st[("ginvc", c)][:, 0:w].bitcast(FP8X4),
-                rhs_scale=st[("ginvs", c)][:, 0:w],
+                out=acc[:],
+                lhsT=st[("ginvc", c)][:, cols].bitcast(FP8X4),
+                lhsT_scale=st[("ginvs", c)][:, cols],
+                rhs=xxc[:, rows].bitcast(FP8X4),
+                rhs_scale=xxs[:, rows],
                 start=True,
                 stop=False,
             )
             nc.tensor.matmul_mx(
-                out=acc[:, 0:w],
-                lhsT=xc[:, cols].bitcast(FP8X4),
-                lhsT_scale=xs[:, cols],
-                rhs=st[("gqc", c)][:, 0:w].bitcast(FP8X4),
-                rhs_scale=st[("gqs", c)][:, 0:w],
+                out=acc[:],
+                lhsT=st[("gqc", c)][:, cols].bitcast(FP8X4),
+                lhsT_scale=st[("gqs", c)][:, cols],
+                rhs=xc[:, rows].bitcast(FP8X4),
+                rhs_scale=xs[:, rows],
                 start=False,
                 stop=True,
             )
-
-        def adds(c, h):
-            w = len(tiles_of(c)) * P
-            z4 = work.tile([P, QN, CT * P], F32, tag="z4", bufs=2, name="z4")
-            st[("z4", c, h)] = z4
-            for j in range(QN):
-                n = QN * h + j
-                nc.vector.scalar_tensor_tensor(
-                    out=z4[:, j, 0:w],
-                    in0=st[("acc", c, n)][:, 0:w],
-                    scalar=-2.0,
-                    in1=st[("cb", c)][:, 0:w],
-                    op0=ALU.mult,
-                    op1=ALU.add,
-                )
-                mm(c, n + 3)
-
-        def zmax(c, h):
-            w = len(tiles_of(c)) * P
-            z4 = st[("z4", c, h)]
-            e4 = work.tile([P, QN, CT * P], F32, tag="e4", bufs=3, name="e4")
-            st[("e4", c, h)] = e4
-            nc.vector.tensor_reduce(
-                out=neg_m[:, c, QN * h : QN * (h + 1)], in_=z4[:, :, 0:w], axis=AX.X, op=ALU.max, negate=True
+            nc.scalar.activation(
+                out=st[("zt", u)][:, i, :], in_=acc[:], func=ACT.Identity, scale=-2.0, bias=st[("cv", c)][:, i : i + 1]
             )
+
+        def z_turn(u):
+            c, h = divmod(u, 2)
+            nt = len(tiles_of(c))
+            for j in range(QN):
+                zz = psum.tile([P, CT * P], F32, tag="zz", bufs=4, name="zz")
+                st[("zz", u, j)] = zz
+                for i in range(nt):
+                    nc.tensor.transpose(zz[:, i * P : (i + 1) * P], st[("zt", u)][:, i, j * P : (j + 1) * P], ident_f[:])
+
+        def soft(u):
+            c, h = divmod(u, 2)
+            w = len(tiles_of(c)) * P
+            e4 = work.tile([P, QN, CT * P], F32, tag="e4", name="e4")
+            st[("e4", u)] = e4
             for j in range(QN):
                 n = QN * h + j
-                nc.scalar.activation(
-                    out=e4[:, j, 0:w], in_=z4[:, j, 0:w], func=ACT.Exp, bias=neg_m[:, c, n : n + 1]
-                )
+                zz = st[("zz", u, j)]
+                nc.vector.tensor_reduce(out=neg_m[:, c, n : n + 1], in_=zz[:, 0:w], axis=AX.X, op=ALU.max, negate=True)
+                nc.scalar.activation(out=e4[:, j, 0:w], in_=zz[:, 0:w], func=ACT.Exp, bias=neg_m[:, c, n : n + 1])
 
-        def fold(c, h):
-            w = len(tiles_of(c)) * P
-            e4 = st[("e4", c, h)]
-            for half in (w // 2, w // 4):
-                nc.gpsimd.tensor_tensor(
-                    out=e4[:, :, 0:half], in0=e4[:, :, 0:half], in1=e4[:, :, half : 2 * half], op=ALU.add
-                )
-
-        def class_sum(c, h):
+        def class_sum(u):
+            c, h = divmod(u, 2)
             w = len(tiles_of(c)) * P
             nc.vector.tensor_reduce(
                 out=s_cls[:, QN * h : QN * (h + 1), c, 0 : w // KC],
-                in_=st[("e4", c, h)][:, :, 0 : w // 4].rearrange("p j (c l) -> p j c l", l=4),
+                in_=st[("e4", u)][:, :, 0:w].rearrange("p j (c k) -> p j c k", k=KC),
                 axis=AX.X,
                 op=ALU.add,
             )
+            if h == 1:
+                nc.vector.tensor_reduce(out=s_sum[:, c, :], in_=s_cls[:, :, c, :], axis=AX.X, op=ALU.add)
 
-        def chunk_sum(c):
-            nc.vector.tensor_reduce(out=s_sum[:, c, :], in_=s_cls[:, :, c, :], axis=AX.X, op=ALU.add)
+        for u in range(-4, NU + 1):
+            flush()
+            if u % 2 == 1 and 0 <= (u + 1) // 2 < NCH:
+                quantise((u + 1) // 2, "gq")
+            if 0 <= u < NU:
+                z_turn(u)
+            if 0 <= u - 1 < NU:
+                class_sum(u - 1)
+            if 0 <= u < NU:
+                soft(u)
+            pc = (u + 3) // 2 if u % 2 == 1 else (u + 2) // 2
+            turner = turn_inv if u % 2 == 1 else turn_q
+            has_prep = 0 <= pc < NCH
+            if has_prep:
+                turner(pc, 0)
+                turner(pc, 1)
+            if 0 <= u + 1 < NU:
+                for i in range(CT):
+                    products(u + 1, i)
+            if has_prep:
+                turner(pc, 2)
+                turner(pc, 3)
+                if u % 2 == 1:
+                    make_q(pc)
+                else:
+                    row_sums(pc)
+                    quantise(pc, "ginv")
+            if u % 2 == 0:
+                invert((u + 4) // 2)
 
-        invert(0)
-        make_q(0)
-        for c in range(-1, NCH):
-            p = c + 1
-            has_main = c >= 0
-            has_prep = p < NCH
-
-            def prep(f, *args):
-                if has_prep:
-                    f(p, *args)
-
-            def main(f, *args):
-                if has_main:
-                    f(c, *args)
-
-            for i in range(CT):
-                prep(turn_inv, i)
-            if c == -1:
-                invert(1)
-            else:
-                make_q(c + 2)
-            for n in range(3):
-                main(mm, n)
-            main(adds, 0)
-            prep(row_sum, 0)
-            prep(row_sum, 1)
-            main(zmax, 0)
-            main(fold, 0)
-            for i in range(CT):
-                prep(turn_q, i)
-            main(adds, 1)
-            prep(row_sum, 2)
-            prep(row_sum, 3)
-            prep(const_vec)
-            main(zmax, 1)
-            main(fold, 1)
-            prep(const_spread)
-            if c >= 1:
-                class_sum(c - 1, 1)
-                chunk_sum(c - 1)
-            prep(quantise, "ginv")
-            prep(quantise, "gq")
-            if c == -1:
-                make_q(1)
-            main(class_sum, 0)
-            invert(c + 3)
-
-        class_sum(NCH - 1, 1)
-        chunk_sum(NCH - 1)
         g_min = keep.tile([P, NB], F32)
         dd = keep.tile([P, NCH, NB], F32)
         ft = keep.tile([P, NCH, NB], F32)

@@ -39,7 +39,6 @@ def tile_dgmmc_diagonal_kernel(tc, x, means, bandwidths, weights, priors, out):
     with ExitStack() as ctx:
         keep = ctx.enter_context(tc.tile_pool(name="keep", bufs=1))
         psum = ctx.enter_context(tc.psum_pool(name="psum", bufs=1))
-        ctx.enter_context(tc.manual_schedule())
 
         def tiles_of(c):
             return range(c * CT, min(NT, (c + 1) * CT))
@@ -193,6 +192,8 @@ def tile_dgmmc_diagonal_kernel(tc, x, means, bandwidths, weights, priors, out):
                 out=ldw[:], in0=ld[:], scalar=-0.5, in1=lw2t[:], op0=ALU.mult, op1=ALU.add
             )
 
+        zero_t = keep.tile([P, 1], F32)
+        nc.vector.tensor_scalar(out=zero_t[:], in0=ldw[:, 0:1], scalar1=0.0, scalar2=None, op0=ALU.mult)
         work = ctx.enter_context(tc.tile_pool(name="work", bufs=2))
 
         st = {}
@@ -205,7 +206,9 @@ def tile_dgmmc_diagonal_kernel(tc, x, means, bandwidths, weights, priors, out):
 
         def invert(c):
             if 0 <= c < NCH:
-                nc.scalar.activation(out=binv[:, span(c), :], in_=binv[:, span(c), :], func=ACT.Exp, scale=-1.0)
+                nc.scalar.activation(
+                    out=binv[:, span(c), :], in_=binv[:, span(c), :], func=ACT.Exp, scale=-1.0, bias=zero_t[:]
+                )
 
         def turn(i, src, dst, late):
             tp = psum.tile([P, 4, P], F32, tag="tp", bufs=2, name="tp")
@@ -213,7 +216,7 @@ def tile_dgmmc_diagonal_kernel(tc, x, means, bandwidths, weights, priors, out):
                 nc.tensor.transpose(tp[:, t, :], src[:, t * P : (t + 1) * P], ident_f[:])
 
             def evac():
-                nc.scalar.copy(out=dst[:, i * P : (i + 1) * P, :], in_=tp[:].rearrange("p t r -> p r t"))
+                nc.any.tensor_copy(out=dst[:, i * P : (i + 1) * P, :], in_=tp[:].rearrange("p t r -> p r t"))
 
             if late:
                 st["pending"].append(evac)
@@ -277,7 +280,7 @@ def tile_dgmmc_diagonal_kernel(tc, x, means, bandwidths, weights, priors, out):
             if i >= len(tiles_of(c)):
                 return
             if i == 0:
-                st[("zt", u)] = work.tile([P, CT, QN * P], F32, tag="zt", name="zt")
+                st[("zt", u)] = work.tile([P, CT, QN * P], F32, tag="zt", bufs=3, name="zt")
             rows = slice(h * QN * P, (h + 1) * QN * P)
             cols = slice(i * P, (i + 1) * P)
             acc = psum.tile([P, QN * P], F32, tag="acc", bufs=2, name="acc")
@@ -299,8 +302,13 @@ def tile_dgmmc_diagonal_kernel(tc, x, means, bandwidths, weights, priors, out):
                 start=False,
                 stop=True,
             )
-            nc.scalar.activation(
-                out=st[("zt", u)][:, i, :], in_=acc[:], func=ACT.Identity, scale=-2.0, bias=st[("cv", c)][:, i : i + 1]
+            nc.any.tensor_scalar(
+                out=st[("zt", u)][:, i, :],
+                in0=acc[:],
+                scalar1=-2.0,
+                scalar2=st[("cv", c)][:, i : i + 1],
+                op0=ALU.mult,
+                op1=ALU.add,
             )
 
         def z_turn(u):
@@ -315,7 +323,7 @@ def tile_dgmmc_diagonal_kernel(tc, x, means, bandwidths, weights, priors, out):
         def soft(u):
             c, h = divmod(u, 2)
             w = len(tiles_of(c)) * P
-            e4 = work.tile([P, QN, CT * P], F32, tag="e4", name="e4")
+            e4 = work.tile([P, QN, CT * P], F32, tag="e4", bufs=3, name="e4")
             st[("e4", u)] = e4
             for j in range(QN):
                 n = QN * h + j

@@ -193,6 +193,8 @@ def tile_dgmmc_diagonal_kernel(tc, x, means, bandwidths, weights, priors, out):
             )
 
         zero_t = keep.tile([P, 1], F32)
+        warm = keep.tile([P, 2], F32)
+        nc.scalar.activation(out=warm[:, 0:1], in_=ld[:, NT - 1 : NT], func=ACT.Exp, scale=0.0)
         nc.vector.tensor_scalar(out=zero_t[:], in0=ldw[:, 0:1], scalar1=0.0, scalar2=None, op0=ALU.mult)
         work = ctx.enter_context(tc.tile_pool(name="work", bufs=2))
 
@@ -205,7 +207,10 @@ def tile_dgmmc_diagonal_kernel(tc, x, means, bandwidths, weights, priors, out):
             st["pending"] = []
 
         def invert(c):
-            if 0 <= c < NCH:
+            if c == 0:
+                for t in tiles_of(c):
+                    nc.scalar.activation(out=binv[:, t, :], in_=binv[:, t, :], func=ACT.Exp, scale=-1.0, bias=zero_t[:])
+            elif 0 < c < NCH:
                 nc.scalar.activation(
                     out=binv[:, span(c), :], in_=binv[:, span(c), :], func=ACT.Exp, scale=-1.0, bias=zero_t[:]
                 )
@@ -241,9 +246,13 @@ def tile_dgmmc_diagonal_kernel(tc, x, means, bandwidths, weights, priors, out):
             ts = tiles_of(c)
             q = work.tile([P, CT, D], F32, tag="q", name="q")
             st[("q", c)] = q
-            nc.vector.tensor_tensor(
-                out=q[:, 0 : len(ts), :], in0=m_raw[:, span(c), :], in1=binv[:, span(c), :], op=ALU.mult
-            )
+            if c == 0:
+                for i in range(len(ts)):
+                    nc.vector.tensor_tensor(out=q[:, i, :], in0=m_raw[:, ts[i], :], in1=binv[:, ts[i], :], op=ALU.mult)
+            else:
+                nc.vector.tensor_tensor(
+                    out=q[:, 0 : len(ts), :], in0=m_raw[:, span(c), :], in1=binv[:, span(c), :], op=ALU.mult
+                )
 
         def row_sums(c):
             ts = tiles_of(c)
@@ -283,7 +292,7 @@ def tile_dgmmc_diagonal_kernel(tc, x, means, bandwidths, weights, priors, out):
                 st[("zt", u)] = work.tile([P, CT, QN * P], F32, tag="zt", bufs=3, name="zt")
             rows = slice(h * QN * P, (h + 1) * QN * P)
             cols = slice(i * P, (i + 1) * P)
-            acc = psum.tile([P, QN * P], F32, tag="acc", bufs=2, name="acc")
+            acc = psum.tile([P, QN * P], F32, tag="acc", bufs=3, name="acc")
             nc.tensor.matmul_mx(
                 out=acc[:],
                 lhsT=st[("ginvc", c)][:, cols].bitcast(FP8X4),
@@ -315,7 +324,7 @@ def tile_dgmmc_diagonal_kernel(tc, x, means, bandwidths, weights, priors, out):
             c, h = divmod(u, 2)
             nt = len(tiles_of(c))
             for j in range(QN):
-                zz = psum.tile([P, CT * P], F32, tag="zz", bufs=4, name="zz")
+                zz = psum.tile([P, CT * P], F32, tag="zz", bufs=3, name="zz")
                 st[("zz", u, j)] = zz
                 for i in range(nt):
                     nc.tensor.transpose(zz[:, i * P : (i + 1) * P], st[("zt", u)][:, i, j * P : (j + 1) * P], ident_f[:])
@@ -384,6 +393,7 @@ def tile_dgmmc_diagonal_kernel(tc, x, means, bandwidths, weights, priors, out):
             out=dd[:], in0=g_min[:].unsqueeze(1).to_broadcast([P, NCH, NB]), in1=neg_m[:], op=ALU.subtract
         )
         nc.scalar.activation(out=dd[:], in_=dd[:], func=ACT.Exp)
+        nc.scalar.activation(out=warm[:, 1:2], in_=dd[:, 0, 0:1], func=ACT.Ln, bias=eps_t[:])
         nc.vector.tensor_tensor(out=ft[:], in0=dd[:], in1=s_sum[:], op=ALU.mult)
         nc.vector.tensor_reduce(out=tot[:], in_=ft[:].rearrange("p c n -> p n c"), axis=AX.X, op=ALU.add)
         nc.vector.reciprocal(out=rec[:], in_=tot[:])

@@ -101,7 +101,8 @@ def tile_dgmmc_diagonal_kernel(tc, x, means, bandwidths, weights, priors, out):
             w_max = early.tile([P, G8], F32)
             w_sum = early.tile([P, G8], F32)
             w_rec = early.tile([P, G8], F32)
-            pr_bc = early.tile([P, NCLS], BF16)
+            pr_row = early.tile([P, 2 * P], BF16)
+            ones_b = early.tile([P, P], BF16)
             pr_e = early.tile([P, NCLS], F32)
             pr_nmax = early.tile([P, 1], F32)
             pr_sum = early.tile([P, 1], F32)
@@ -110,6 +111,8 @@ def tile_dgmmc_diagonal_kernel(tc, x, means, bandwidths, weights, priors, out):
             pr_tf = early.tile([P, G8], F32)
             lwp = early.tile([P, G8, KC], F32)
 
+            nc.gpsimd.memset(pr_row[:], 0.0)
+            nc.gpsimd.memset(ones_b[:], 1.0)
             nc.gpsimd.memset(lwp[:], 0.0)
             make_identity(nc, ident_b[:])
             make_identity(nc, ident_f[:])
@@ -117,22 +120,24 @@ def tile_dgmmc_diagonal_kernel(tc, x, means, bandwidths, weights, priors, out):
             nc.vector.memset(tiny_t[:], 2.0 ** -63)
 
             nc.scalar.dma_start(out=w_sb[0:NT], in_=weights.rearrange("(t c k) -> t c k", c=G8, k=KC))
-            nc.scalar.dma_start(out=pr_bc[:], in_=priors.partition_broadcast(P))
+            nc.scalar.dma_start(out=pr_row[0:1, 0:NCLS], in_=priors.rearrange("(o c) -> o c", o=1))
             nc.scalar.dma_start(out=pr_t[0:NT], in_=priors.rearrange("(t c) -> t c", c=G8))
 
             load_bw(0)
             load_bw(1)
-            nc.sync.dma_start(out=x_raw[:], in_=x.rearrange("(n p) d -> p n d", p=P))
             load_bw(2)
+            nc.sync.dma_start(out=x_raw[:], in_=x.rearrange("(n p) d -> p n d", p=P))
 
             R = NT
             nc.vector.tensor_reduce(out=w_max[0:R], in_=w_sb[0:R], axis=AX.X, op=ALU.max)
             nc.vector.tensor_tensor(
                 out=w_f[0:R], in0=w_sb[0:R], in1=w_max[0:R].unsqueeze(2).to_broadcast([R, G8, KC]), op=ALU.subtract
             )
-            nc.vector.tensor_reduce(out=pr_nmax[:], in_=pr_bc[:], axis=AX.X, op=ALU.max, negate=True)
+            pr_bc = psum.tile([P, 2 * P], F32, tag="tp", bufs=2, name="pr_bc")
+            nc.tensor.matmul(out=pr_bc[:], lhsT=ones_b[:], rhs=pr_row[:], start=True, stop=True)
+            nc.vector.tensor_reduce(out=pr_nmax[:], in_=pr_bc[:, 0:NCLS], axis=AX.X, op=ALU.max, negate=True)
             nc.scalar.activation(out=w_f[0:R], in_=w_f[0:R], func=ACT.Exp)
-            nc.scalar.activation(out=pr_e[:], in_=pr_bc[:], func=ACT.Exp, bias=pr_nmax[:], accum_out=pr_sum[:])
+            nc.scalar.activation(out=pr_e[:], in_=pr_bc[:, 0:NCLS], func=ACT.Exp, bias=pr_nmax[:], accum_out=pr_sum[:])
             nc.scalar.activation(out=pr_tf[0:R], in_=pr_t[0:R], func=ACT.Exp, bias=pr_nmax[0:R])
             for i in range(CT):
                 clip(0, i, i + 1)

from contextlib import ExitStack
import math

import concourse.mybir as mybir
from concourse.masks import make_identity

F32 = mybir.dt.float32
BF16 = mybir.dt.bfloat16
U32 = mybir.dt.uint32
U8 = mybir.dt.uint8
FP8X4 = mybir.dt.float8_e4m3fn_x4
ALU = mybir.AluOpType
ACT = mybir.ActivationFunctionType
AX = mybir.AxisListType

P = 128
D = 512
B = 1024
NCOMP = 3200
NCLS = 200
KC = 16
NB = B // P
NT = NCOMP // P
CT = 4
NCH = (NT + CT - 1) // CT
CCH = CT * P // KC
G8 = P // KC
LOG_2PI = math.log(2.0 * math.pi)
UP = 2.0 ** 60
FLOPS = 2 * 2 * B * NCOMP * D

CLIP_ON_POOL = False
QN = 4
NU = 2 * NCH


def tile_dgmmc_diagonal_kernel(tc, x, means, bandwidths, weights, priors, out):
    nc = tc.nc
    with ExitStack() as ctx:
        keep = ctx.enter_context(tc.tile_pool(name="keep", bufs=1))
        psum = ctx.enter_context(tc.psum_pool(name="psum", bufs=1))

        def tiles_of(c):
            return range(c * CT, min(NT, (c + 1) * CT))

        def span(c):
            ts = tiles_of(c)
            return slice(ts[0], ts[-1] + 1)

        ident_f = keep.tile([P, P], F32)
        ident_b = keep.tile([P, P], BF16)
        m_raw = keep.tile([P, NT, D], BF16)
        binv = keep.tile([P, NT, D], F32)
        xc = keep.tile([P, B], U32, align_bytes=64)
        xs = keep.tile([P, B], U8, align_bytes=64)
        xxc = keep.tile([P, B], U32, align_bytes=64)
        xxs = keep.tile([P, B], U8, align_bytes=64)
        ld = keep.tile([P, NT], F32)
        s_m = keep.tile([P, NT], F32)
        lw2t = keep.tile([P, NT], F32)
        ldw = keep.tile([P, NT], F32)
        junk = keep.tile([P, D], F32)
        neg_m = keep.tile([P, NCH, NB], F32)
        s_sum = keep.tile([P, NCH, NB], F32)
        s_cls = keep.tile([P, NB, NCH, CCH], F32)
        res = keep.tile([P, NB, NCLS], F32)
        eps_t = keep.tile([P, 1], F32)
        tiny_t = keep.tile([P, 1], F32)

        bw_v = bandwidths.rearrange("(t p) d -> p t d", p=P)
        m_v = means.rearrange("(t p) d -> p t d", p=P)
        bw_t = {}

        def load_bw(c):
            bw_t[c] = keep.tile([P, CT, D], BF16, tag="bw", bufs=3, name="bw")
            nc.sync.dma_start(out=bw_t[c][:, 0 : len(tiles_of(c)), :], in_=bw_v[:, span(c), :])

        def clip(c, i0, i1):
            ts = tiles_of(c)
            i1 = min(i1, len(ts))
            eng = nc.gpsimd if CLIP_ON_POOL else nc.vector
            eng.tensor_scalar(
                out=binv[:, ts[0] + i0 : ts[0] + i1, :],
                in0=bw_t[c][:, i0:i1, :],
                scalar1=1000.0,
                scalar2=1.0e-6,
                op0=ALU.min,
                op1=ALU.max,
            )

        def logs(c):
            for t in tiles_of(c):
                nc.scalar.activation(out=binv[:, t, :], in_=binv[:, t, :], func=ACT.Ln, accum_out=ld[:, t : t + 1])

        with tc.tile_pool(name="early", bufs=1) as early:
            x_raw = early.tile([P, NB, D], BF16)
            xg = early.tile([P, NB, P, 4], BF16, align_bytes=64)
            xxg = early.tile([P, NB, P, 4], BF16, align_bytes=64)
            w_sb = early.tile([P, G8, KC], BF16)
            w_f = early.tile([P, G8, KC], F32)
            w_max = early.tile([P, G8], F32)
            w_sum = early.tile([P, G8], F32)
            w_rec = early.tile([P, G8], F32)
            pr_row = early.tile([P, 2 * P], BF16)
            ones_b = early.tile([P, P], BF16)
            pr_e = early.tile([P, NCLS], F32)
            pr_nmax = early.tile([P, 1], F32)
            pr_sum = early.tile([P, 1], F32)
            pr_rec = early.tile([P, 1], F32)
            pr_t = early.tile([P, G8], BF16)
            pr_tf = early.tile([P, G8], F32)
            lwp = early.tile([P, G8, KC], F32)

            nc.gpsimd.memset(pr_row[:], 0.0)
            nc.gpsimd.memset(ones_b[:], 1.0)
            nc.gpsimd.memset(lwp[:], 0.0)
            make_identity(nc, ident_b[:])
            make_identity(nc, ident_f[:])
            nc.vector.memset(eps_t[:], 1.0e-6)
            nc.vector.memset(tiny_t[:], 2.0 ** -63)

            nc.scalar.dma_start(out=w_sb[0:NT], in_=weights.rearrange("(t c k) -> t c k", c=G8, k=KC))
            nc.scalar.dma_start(out=pr_row[0:1, 0:NCLS], in_=priors.rearrange("(o c) -> o c", o=1))
            nc.scalar.dma_start(out=pr_t[0:NT], in_=priors.rearrange("(t c) -> t c", c=G8))

            load_bw(0)
            load_bw(1)
            load_bw(2)
            nc.sync.dma_start(out=x_raw[:], in_=x.rearrange("(n p) d -> p n d", p=P))

            R = NT
            nc.vector.tensor_reduce(out=w_max[0:R], in_=w_sb[0:R], axis=AX.X, op=ALU.max)
            nc.vector.tensor_tensor(
                out=w_f[0:R], in0=w_sb[0:R], in1=w_max[0:R].unsqueeze(2).to_broadcast([R, G8, KC]), op=ALU.subtract
            )
            pr_bc = psum.tile([P, 2 * P], F32, tag="tp", bufs=2, name="pr_bc")
            nc.tensor.matmul(out=pr_bc[:], lhsT=ones_b[:], rhs=pr_row[:], start=True, stop=True)
            nc.vector.tensor_reduce(out=pr_nmax[:], in_=pr_bc[:, 0:NCLS], axis=AX.X, op=ALU.max, negate=True)
            nc.scalar.activation(out=w_f[0:R], in_=w_f[0:R], func=ACT.Exp)
            nc.scalar.activation(out=pr_e[:], in_=pr_bc[:, 0:NCLS], func=ACT.Exp, bias=pr_nmax[:], accum_out=pr_sum[:])
            nc.scalar.activation(out=pr_tf[0:R], in_=pr_t[0:R], func=ACT.Exp, bias=pr_nmax[0:R])
            for i in range(CT):
                clip(0, i, i + 1)
            logs(0)
            nc.vector.tensor_reduce(out=w_sum[0:R], in_=w_f[0:R], axis=AX.X, op=ALU.add)
            nc.vector.reciprocal(out=w_rec[0:R], in_=w_sum[0:R])
            nc.vector.tensor_tensor(
                out=w_f[0:R], in0=w_f[0:R], in1=w_rec[0:R].unsqueeze(2).to_broadcast([R, G8, KC]), op=ALU.mult
            )
            nc.vector.reciprocal(out=pr_rec[:], in_=pr_sum[:])
            nc.vector.tensor_scalar(out=pr_tf[0:R], in0=pr_tf[0:R], scalar1=pr_rec[0:R], scalar2=None, op0=ALU.mult)

            nc.scalar.activation(out=w_f[0:R], in_=w_f[0:R], func=ACT.Ln, bias=eps_t[0:R])
            nc.scalar.activation(out=pr_tf[0:R], in_=pr_tf[0:R], func=ACT.Ln, bias=eps_t[0:R])

            def next_logs(c):
                clip(c, 0, CT)
                if c + 2 < NCH:
                    load_bw(c + 2)
                logs(c)

            def x_turn(n):
                xt = psum.tile([P, 4, P], BF16, tag="tp", bufs=2, name="xt")
                for t in range(4):
                    nc.tensor.transpose(xt[:, t, :], x_raw[:, n, t * P : (t + 1) * P], ident_b[:])
                nc.vector.tensor_scalar(
                    out=xg[:, n, :, :], in0=xt[:].rearrange("p t r -> p r t"), scalar1=-0.5, scalar2=None, op0=ALU.mult
                )

            xg_flat = xg[:].rearrange("p n r t -> p (n r t)")
            xxg_flat = xxg[:].rearrange("p n r t -> p (n r t)")
            next_logs(1)
            next_logs(2)
            for n in range(0, 4):
                x_turn(n)
            next_logs(3)
            for n in range(4, 8):
                x_turn(n)
            next_logs(4)
            next_logs(5)
            for c in range(NCH):
                nc.sync.dma_start(out=m_raw[:, span(c), :], in_=m_v[:, span(c), :])
            nc.vector.tensor_tensor(out=xxg_flat, in0=xg_flat, in1=xg_flat, op=ALU.mult)
            next_logs(6)
            nc.vector.quantize_mx(out=xc[:].bitcast(FP8X4), scales=xs[:], in_=xg_flat)
            nc.vector.tensor_tensor(
                out=lwp[0:R], in0=w_f[0:R], in1=pr_tf[0:R].unsqueeze(2).to_broadcast([R, G8, KC]), op=ALU.add
            )
            lt = psum.tile([P, P], F32, tag="tp", bufs=2, name="lt")
            nc.tensor.transpose(lt[:], lwp[:].rearrange("p c k -> p (c k)"), ident_f[:])
            nc.vector.quantize_mx(out=xxc[:].bitcast(FP8X4), scales=xxs[:], in_=xxg_flat)
            nc.vector.tensor_scalar(
                out=lw2t[:], in0=lt[:, 0:NT], scalar1=-0.5 * D * LOG_2PI, scalar2=None, op0=ALU.add
            )
            nc.gpsimd.memset(s_cls[:], 0.0)
            nc.vector.scalar_tensor_tensor(
                out=ldw[:], in0=ld[:], scalar=-0.5, in1=lw2t[:], op0=ALU.mult, op1=ALU.add
            )

        zero_t = keep.tile([P, 1], F32)
        warm = keep.tile([P, 2], F32)
        nc.scalar.activation(out=warm[:, 0:1], in_=ld[:, NT - 1 : NT], func=ACT.Exp, scale=0.0)
        nc.vector.tensor_scalar(out=zero_t[:], in0=ldw[:, 0:1], scalar1=0.0, scalar2=None, op0=ALU.mult)
        work = ctx.enter_context(tc.tile_pool(name="work", bufs=2))

        st = {}
        st["pending"] = []

        def flush():
            for f in st["pending"]:
                f()
            st["pending"] = []

        def invert(c):
            if c == 0:
                for t in tiles_of(c):
                    nc.scalar.activation(out=binv[:, t, :], in_=binv[:, t, :], func=ACT.Exp, scale=-1.0, bias=zero_t[:])
            elif 0 < c < NCH:
                nc.scalar.activation(
                    out=binv[:, span(c), :], in_=binv[:, span(c), :], func=ACT.Exp, scale=-1.0, bias=zero_t[:]
                )

        def turn(i, src, dst, late):
            tp = psum.tile([P, 4, P], F32, tag="tp", bufs=2, name="tp")
            for t in range(4):
                nc.tensor.transpose(tp[:, t, :], src[:, t * P : (t + 1) * P], ident_f[:])

            def evac():
                nc.any.tensor_copy(out=dst[:, i * P : (i + 1) * P, :], in_=tp[:].rearrange("p t r -> p r t"))

            if late:
                st["pending"].append(evac)
            else:
                evac()

        def turn_inv(c, i):
            ts = tiles_of(c)
            if i == 0:
                st[("ginv", c)] = work.tile([P, CT * P, 4], BF16, tag="ginv", align_bytes=64, name="ginv")
            if i < len(ts):
                turn(i, binv[:, ts[i], :], st[("ginv", c)], i >= 2)

        def turn_q(c, i):
            ts = tiles_of(c)
            if i == 0:
                st[("gq", c)] = work.tile([P, CT * P, 4], BF16, tag="gq", align_bytes=64, name="gq")
            if i < len(ts):
                turn(i, st[("q", c)][:, i, :], st[("gq", c)], i >= 2)

        def make_q(c):
            ts = tiles_of(c)
            q = work.tile([P, CT, D], F32, tag="q", name="q")
            st[("q", c)] = q
            if c == 0:
                for i in range(len(ts)):
                    nc.vector.tensor_tensor(out=q[:, i, :], in0=m_raw[:, ts[i], :], in1=binv[:, ts[i], :], op=ALU.mult)
            else:
                nc.vector.tensor_tensor(
                    out=q[:, 0 : len(ts), :], in0=m_raw[:, span(c), :], in1=binv[:, span(c), :], op=ALU.mult
                )

        def row_sums(c):
            ts = tiles_of(c)
            for i in range(len(ts)):
                nc.vector.scalar_tensor_tensor(
                    out=junk[:],
                    in0=st[("q", c)][:, i, :],
                    scalar=1.0,
                    in1=m_raw[:, ts[i], :],
                    op0=ALU.mult,
                    op1=ALU.mult,
                    accum_out=s_m[:, ts[i] : ts[i] + 1],
                )
            cv = work.tile([P, CT], F32, tag="cv", name="cv")
            st[("cv", c)] = cv
            nc.vector.scalar_tensor_tensor(
                out=cv[:, 0 : len(ts)], in0=s_m[:, span(c)], scalar=-0.5, in1=ldw[:, span(c)], op0=ALU.mult, op1=ALU.add
            )

        def quantise(c, key):
            w = len(tiles_of(c)) * P
            codes = work.tile([P, CT * P], U32, tag=key + "c", align_bytes=64, name=key + "c")
            scales = work.tile([P, CT * P], U8, tag=key + "s", align_bytes=64, name=key + "s")
            st[(key + "c", c)] = codes
            st[(key + "s", c)] = scales
            nc.vector.quantize_mx(
                out=codes[:, 0:w].bitcast(FP8X4),
                scales=scales[:, 0:w],
                in_=st[(key, c)][:, 0:w, :].rearrange("p r t -> p (r t)"),
            )

        def products(u, i):
            c, h = divmod(u, 2)
            if i >= len(tiles_of(c)):
                return
            if i == 0:
                st[("zt", u)] = work.tile([P, CT, QN * P], F32, tag="zt", bufs=3, name="zt")
            rows = slice(h * QN * P, (h + 1) * QN * P)
            cols = slice(i * P, (i + 1) * P)
            acc = psum.tile([P, QN * P], F32, tag="acc", bufs=3, name="acc")
            nc.tensor.matmul_mx(
                out=acc[:],
                lhsT=st[("ginvc", c)][:, cols].bitcast(FP8X4),
                lhsT_scale=st[("ginvs", c)][:, cols],
                rhs=xxc[:, rows].bitcast(FP8X4),
                rhs_scale=xxs[:, rows],
                start=True,
                stop=False,
            )
            nc.tensor.matmul_mx(
                out=acc[:],
                lhsT=st[("gqc", c)][:, cols].bitcast(FP8X4),
                lhsT_scale=st[("gqs", c)][:, cols],
                rhs=xc[:, rows].bitcast(FP8X4),
                rhs_scale=xs[:, rows],
                start=False,
                stop=True,
            )
            nc.any.tensor_scalar(
                out=st[("zt", u)][:, i, :],
                in0=acc[:],
                scalar1=-2.0,
                scalar2=st[("cv", c)][:, i : i + 1],
                op0=ALU.mult,
                op1=ALU.add,
            )

        def z_turn(u):
            c, h = divmod(u, 2)
            nt = len(tiles_of(c))
            for j in range(QN):
                zz = psum.tile([P, CT * P], F32, tag="zz", bufs=3, name="zz")
                st[("zz", u, j)] = zz
                for i in range(nt):
                    nc.tensor.transpose(zz[:, i * P : (i + 1) * P], st[("zt", u)][:, i, j * P : (j + 1) * P], ident_f[:])

        def soft(u):
            c, h = divmod(u, 2)
            w = len(tiles_of(c)) * P
            e4 = work.tile([P, QN, CT * P], F32, tag="e4", bufs=3, name="e4")
            st[("e4", u)] = e4
            for j in range(QN):
                n = QN * h + j
                zz = st[("zz", u, j)]
                nc.vector.tensor_reduce(out=neg_m[:, c, n : n + 1], in_=zz[:, 0:w], axis=AX.X, op=ALU.max, negate=True)
                nc.scalar.activation(out=e4[:, j, 0:w], in_=zz[:, 0:w], func=ACT.Exp, bias=neg_m[:, c, n : n + 1])

        def class_sum(u):
            c, h = divmod(u, 2)
            w = len(tiles_of(c)) * P
            nc.vector.tensor_reduce(
                out=s_cls[:, QN * h : QN * (h + 1), c, 0 : w // KC],
                in_=st[("e4", u)][:, :, 0:w].rearrange("p j (c k) -> p j c k", k=KC),
                axis=AX.X,
                op=ALU.add,
            )
            if h == 1:
                nc.vector.tensor_reduce(out=s_sum[:, c, :], in_=s_cls[:, :, c, :], axis=AX.X, op=ALU.add)

        for u in range(-4, NU + 1):
            flush()
            if u % 2 == 1 and 0 <= (u + 1) // 2 < NCH:
                quantise((u + 1) // 2, "gq")
            if 0 <= u < NU:
                z_turn(u)
            if 0 <= u - 1 < NU:
                class_sum(u - 1)
            if 0 <= u < NU:
                soft(u)
            pc = (u + 3) // 2 if u % 2 == 1 else (u + 2) // 2
            turner = turn_inv if u % 2 == 1 else turn_q
            has_prep = 0 <= pc < NCH
            if has_prep:
                turner(pc, 0)
                turner(pc, 1)
            if 0 <= u + 1 < NU:
                for i in range(CT):
                    products(u + 1, i)
            if has_prep:
                turner(pc, 2)
                turner(pc, 3)
                if u % 2 == 1:
                    make_q(pc)
                else:
                    row_sums(pc)
                    quantise(pc, "ginv")
            if u % 2 == 0:
                invert((u + 4) // 2)

        g_min = keep.tile([P, NB], F32)
        dd = keep.tile([P, NCH, NB], F32)
        ft = keep.tile([P, NCH, NB], F32)
        tot = keep.tile([P, NB], F32)
        rec = keep.tile([P, NB], F32)
        gg = keep.tile([P, NB, NCH], F32)
        nc.vector.tensor_reduce(out=g_min[:], in_=neg_m[:].rearrange("p c n -> p n c"), axis=AX.X, op=ALU.min)
        nc.vector.tensor_tensor(
            out=dd[:], in0=g_min[:].unsqueeze(1).to_broadcast([P, NCH, NB]), in1=neg_m[:], op=ALU.subtract
        )
        nc.scalar.activation(out=dd[:], in_=dd[:], func=ACT.Exp)
        nc.scalar.activation(out=warm[:, 1:2], in_=dd[:, 0, 0:1], func=ACT.Ln, bias=eps_t[:])
        nc.vector.tensor_tensor(out=ft[:], in0=dd[:], in1=s_sum[:], op=ALU.mult)
        nc.vector.tensor_reduce(out=tot[:], in_=ft[:].rearrange("p c n -> p n c"), axis=AX.X, op=ALU.add)
        nc.vector.reciprocal(out=rec[:], in_=tot[:])
        nc.vector.scalar_tensor_tensor(
            out=gg[:].rearrange("p n c -> p c n"),
            in0=dd[:],
            scalar=UP,
            in1=rec[:].unsqueeze(1).to_broadcast([P, NCH, NB]),
            op0=ALU.mult,
            op1=ALU.mult,
        )
        out_v = out.rearrange("(n p) c -> p n c", p=P)
        H = NB // 2
        for h in range(2):
            ns = slice(h * H, (h + 1) * H)
            sv = s_cls[:, ns, :, :].rearrange("p n c k -> p (n c) k")
            nc.vector.tensor_tensor(
                out=sv,
                in0=sv,
                in1=gg[:, ns, :].rearrange("p n c -> p (n c)").unsqueeze(2).to_broadcast([P, H * NCH, CCH]),
                op=ALU.mult,
            )
            nc.scalar.activation(
                out=res[:, ns, :],
                in_=s_cls[:, ns, :, :].rearrange("p n c k -> p n (c k)")[:, :, 0:NCLS],
                func=ACT.Ln,
                bias=tiny_t[:],
            )
            nc.vector.tensor_scalar(
                out=res[:, ns, :], in0=res[:, ns, :], scalar1=-60.0 * math.log(2.0), scalar2=None, op0=ALU.add
            )
            nc.sync.dma_start(out=out_v[:, ns, :], in_=res[:, ns, :])
